import numpy as np
import ml_dtypes

BF16 = ml_dtypes.bfloat16


def bf(x):
    return np.asarray(x, np.float32).astype(BF16)


def f32(x):
    return np.asarray(x, np.float32)


def f64(x):
    return np.asarray(x).astype(np.float64)


def striped(idx):
    return np.tile(idx.reshape(-1, 16).T, (8, 1))


S, K, H, M, N, PHI = 256, 128, 64, 128, 128, 16


def halfnorm(a):
    q = a.reshape(K // H, H, -1)
    return (q / np.sqrt((q**2).sum(axis=1, keepdims=True))).reshape(K, -1)


def mlp(v, w1, b1, w2, b2):
    return (np.maximum(v[:, :, None] * w1[0] + b1[0], 0.0) * w2[0]).sum(axis=-1) + b2[0, 0]


def setup_inputs():
    return {
        "table": bf(np.random.standard_normal((K, S))),
        "w": bf(np.random.standard_normal((K, M))),
        "fa": f32(np.random.standard_normal((H, 1))),
        "fb": f32(np.random.standard_normal((H, 1))),
        "mlp1_w1": f32(3.0 * np.random.standard_normal((1, PHI))),
        "mlp1_b1": f32(0.3 * np.random.standard_normal((1, PHI))),
        "mlp1_w2": f32(0.5 * np.random.standard_normal((1, PHI))),
        "mlp1_b2": f32(np.random.uniform(0.2, 0.5, (1, 1))),
        "mlp2_w1": f32(1.0 * np.random.standard_normal((1, PHI))),
        "mlp2_b1": f32(0.3 * np.random.standard_normal((1, PHI))),
        "mlp2_w2": f32(0.5 * np.random.standard_normal((1, PHI))),
        "mlp2_b2": f32(np.random.uniform(0.2, 0.5, (1, 1))),
        "offs": striped(np.random.permutation(S)[:N]),
    }


def reference(table, w, fa, fb, mlp1_w1, mlp1_b1, mlp1_w2, mlp1_b2, mlp2_w1, mlp2_b1, mlp2_w2, mlp2_b2, offs):
    idx = offs[:16].T.reshape(-1)
    ft = np.concatenate([f64(fa), f64(fb)], axis=0)
    fw = np.concatenate([f64(fb), f64(fa)], axis=0)
    tn = halfnorm(f64(table) * ft)
    wn = halfnorm(f64(w) * fw)
    x = wn.T @ tn[:, idx]
    h = mlp(x, f64(mlp1_w1), f64(mlp1_b1), f64(mlp1_w2), f64(mlp1_b2))
    return mlp(h, f64(mlp2_w1), f64(mlp2_b1), f64(mlp2_w2), f64(mlp2_b2))

@@ -1,0 +1,118 @@
+import concourse.mybir as mybir
+
+F32 = mybir.dt.float32
+BF16 = mybir.dt.bfloat16
+U16 = mybir.dt.uint16
+ACT = mybir.ActivationFunctionType
+ALU = mybir.AluOpType
+
+K = 128
+H = 64
+S = 256
+M = 128
+N = 128
+PHI = 16
+
+FLOPS = 2 * K * M * N
+
+
+def tile_maa_kernel(
+    tc,
+    table,
+    w,
+    fa,
+    fb,
+    mlp1_w1,
+    mlp1_b1,
+    mlp1_w2,
+    mlp1_b2,
+    mlp2_w1,
+    mlp2_b1,
+    mlp2_w2,
+    mlp2_b2,
+    offs,
+    out,
+):
+    nc = tc.nc
+    with (
+        tc.tile_pool(name="held", bufs=1) as held,
+        tc.tile_pool(name="units", bufs=4) as units,
+        tc.psum_pool(name="psum", bufs=1) as psum,
+    ):
+        table_sb = held.tile([K, S], BF16, name="table_sb")
+        nc.sync.dma_start(table_sb[:], table)
+        w_sb = held.tile([K, M], BF16, name="w_sb")
+        nc.scalar.dma_start(w_sb[:], w)
+
+        ft = held.tile([K, 1], F32, name="ft")
+        nc.sync.dma_start(ft[0:H, :], fa)
+        nc.sync.dma_start(ft[H:K, :], fb)
+        fw = held.tile([K, 1], F32, name="fw")
+        nc.scalar.dma_start(fw[0:H, :], fb)
+        nc.scalar.dma_start(fw[H:K, :], fa)
+
+        offsets = held.tile([128, N // 16], U16, name="offsets")
+        nc.sync.dma_start(offsets[:], offs)
+
+        net = {}
+        for name, row in (
+            ("w1_1", mlp1_w1),
+            ("b1_1", mlp1_b1),
+            ("w2_1", mlp1_w2),
+            ("b2_1", mlp1_b2),
+            ("w1_2", mlp2_w1),
+            ("b1_2", mlp2_b1),
+            ("w2_2", mlp2_w2),
+            ("b2_2", mlp2_b2),
+        ):
+            width = row.shape[1]
+            net[name] = held.tile([M, width], F32, name=name)
+            nc.gpsimd.dma_start(net[name][:], row.broadcast_to([M, width]))
+
+        same_half = held.tile([K, K], BF16, name="same_half")
+        nc.vector.memset(same_half[:], 0.0)
+        nc.vector.memset(same_half[0:H, 0:H], 1.0)
+        nc.vector.memset(same_half[H:K, H:K], 1.0)
+
+        squares = held.tile([K, S + M], BF16, name="squares")
+        nc.scalar.activation(squares[:, 0:S], table_sb[:], ACT.Square, scale=ft[:, 0:1])
+        nc.scalar.activation(squares[:, S : S + M], w_sb[:], ACT.Square, scale=fw[:, 0:1])
+
+        sums = psum.tile([K, S + M], F32, name="sums")
+        nc.tensor.matmul(sums[:], same_half[:], squares[:], start=True, stop=True)
+        inv_norm = held.tile([K, S + M], F32, name="inv_norm")
+        nc.scalar.activation(inv_norm[:], sums[:], ACT.Abs_reciprocal_sqrt)
+
+        tn = held.tile([K, S], BF16, name="tn")
+        nc.vector.scalar_tensor_tensor(
+            tn[:], table_sb[:], ft[:, 0:1], inv_norm[:, 0:S], ALU.mult, ALU.mult
+        )
+        wn = held.tile([K, M], BF16, name="wn")
+        nc.vector.scalar_tensor_tensor(
+            wn[:], w_sb[:], fw[:, 0:1], inv_norm[:, S : S + M], ALU.mult, ALU.mult
+        )
+
+        x = psum.tile([M, N], F32, name="x")
+        nc.tensor.matmul(x[:], wn[:], tn[:].indirect(offsets[:]), start=True, stop=True)
+
+        def network(result, v, w1, b1, w2, b2):
+            for p in range(PHI):
+                unit = units.tile([M, N], F32, name="unit")
+                nc.scalar.activation(
+                    unit[:], v, ACT.Relu, bias=b1[:, p : p + 1], scale=w1[:, p : p + 1]
+                )
+                if p == 0:
+                    nc.vector.tensor_scalar(
+                        result, unit[:], w2[:, 0:1], b2[:, 0:1], ALU.mult, ALU.add
+                    )
+                else:
+                    nc.vector.scalar_tensor_tensor(
+                        result, unit[:], w2[:, p : p + 1], result, ALU.mult, ALU.add
+                    )
+
+        h = held.tile([M, N], F32, name="h")
+        network(h[:], x[:], net["w1_1"], net["b1_1"], net["w2_1"], net["b2_1"])
+        score = held.tile([M, N], F32, name="score")
+        network(score[:], h[:], net["w1_2"], net["b1_2"], net["w2_2"], net["b2_2"])
+
+        nc.sync.dma_start(out, score[:])

@@ -55,19 +55,19 @@ def tile_maa_kernel(
         nc.sync.dma_start(offsets[:], offs)
 
         net = {}
-        for name, row in (
-            ("w1_1", mlp1_w1),
-            ("b1_1", mlp1_b1),
-            ("w2_1", mlp1_w2),
-            ("b2_1", mlp1_b2),
-            ("w1_2", mlp2_w1),
-            ("b1_2", mlp2_b1),
-            ("w2_2", mlp2_w2),
-            ("b2_2", mlp2_b2),
+        for name, row, queue in (
+            ("w1_1", mlp1_w1, nc.sync),
+            ("b1_1", mlp1_b1, nc.scalar),
+            ("w2_1", mlp1_w2, nc.sync),
+            ("b2_1", mlp1_b2, nc.scalar),
+            ("w1_2", mlp2_w1, nc.sync),
+            ("b1_2", mlp2_b1, nc.scalar),
+            ("w2_2", mlp2_w2, nc.sync),
+            ("b2_2", mlp2_b2, nc.scalar),
         ):
             width = row.shape[1]
             net[name] = held.tile([M, width], F32, name=name)
-            nc.gpsimd.dma_start(net[name][:], row.broadcast_to([M, width]))
+            queue.dma_start(net[name][:], row.broadcast_to([M, width]))
 
         same_half = held.tile([K, K], BF16, name="same_half")
         nc.vector.memset(same_half[:], 0.0)

@@ -12,6 +12,7 @@ S = 256
 M = 128
 N = 128
 PHI = 16
+CHAINS = 2
 
 FLOPS = 2 * K * M * N
 
@@ -37,6 +38,7 @@ def tile_maa_kernel(
     with (
         tc.tile_pool(name="held", bufs=1) as held,
         tc.tile_pool(name="units", bufs=4) as units,
+        tc.tile_pool(name="partial", bufs=2) as partial,
         tc.psum_pool(name="psum", bufs=1) as psum,
     ):
         table_sb = held.tile([K, S], BF16, name="table_sb")
@@ -96,19 +98,24 @@ def tile_maa_kernel(
         nc.tensor.matmul(x[:], wn[:], tn[:].indirect(offsets[:]), start=True, stop=True)
 
         def network(result, v, w1, b1, w2, b2):
+            sums = [partial.tile([M, N], F32, name=f"sum{c}") for c in range(CHAINS)]
             for p in range(PHI):
                 unit = units.tile([M, N], F32, name="unit")
                 nc.scalar.activation(
                     unit[:], v, ACT.Relu, bias=b1[:, p : p + 1], scale=w1[:, p : p + 1]
                 )
+                acc = sums[p % CHAINS]
                 if p == 0:
                     nc.vector.tensor_scalar(
-                        result, unit[:], w2[:, 0:1], b2[:, 0:1], ALU.mult, ALU.add
+                        acc[:], unit[:], w2[:, 0:1], b2[:, 0:1], ALU.mult, ALU.add
                     )
+                elif p < CHAINS:
+                    nc.vector.tensor_scalar_mul(acc[:], unit[:], w2[:, p : p + 1])
                 else:
                     nc.vector.scalar_tensor_tensor(
-                        result, unit[:], w2[:, p : p + 1], result, ALU.mult, ALU.add
+                        acc[:], unit[:], w2[:, p : p + 1], acc[:], ALU.mult, ALU.add
                     )
+            nc.vector.tensor_tensor(result, sums[0][:], sums[1][:], ALU.add)
 
         h = held.tile([M, N], F32, name="h")
         network(h[:], x[:], net["w1_1"], net["b1_1"], net["w2_1"], net["b2_1"])

@@ -12,7 +12,8 @@ S = 256
 M = 128
 N = 128
 PHI = 16
-CHAINS = 2
+CHAINS = 4
+PIECE = 128
 
 FLOPS = 2 * K * M * N
 
@@ -37,64 +38,70 @@ def tile_maa_kernel(
     nc = tc.nc
     with (
         tc.tile_pool(name="held", bufs=1) as held,
-        tc.tile_pool(name="units", bufs=4) as units,
+        tc.tile_pool(name="pieces", bufs=3) as pieces,
+        tc.tile_pool(name="units", bufs=6) as units,
         tc.tile_pool(name="partial", bufs=2) as partial,
-        tc.psum_pool(name="psum", bufs=1) as psum,
+        tc.psum_pool(name="psum_sums", bufs=3) as psum_sums,
+        tc.psum_pool(name="psum_x", bufs=1) as psum_x,
     ):
-        table_sb = held.tile([K, S], BF16, name="table_sb")
-        nc.sync.dma_start(table_sb[:], table)
         w_sb = held.tile([K, M], BF16, name="w_sb")
         nc.scalar.dma_start(w_sb[:], w)
-
-        ft = held.tile([K, 1], F32, name="ft")
-        nc.sync.dma_start(ft[0:H, :], fa)
-        nc.sync.dma_start(ft[H:K, :], fb)
         fw = held.tile([K, 1], F32, name="fw")
         nc.scalar.dma_start(fw[0:H, :], fb)
         nc.scalar.dma_start(fw[H:K, :], fa)
+        table_sb = held.tile([K, S], BF16, name="table_sb")
+        nc.sync.dma_start(table_sb[:], table)
+        ft = held.tile([K, 1], F32, name="ft")
+        nc.sync.dma_start(ft[0:H, :], fa)
+        nc.sync.dma_start(ft[H:K, :], fb)
 
         offsets = held.tile([128, N // 16], U16, name="offsets")
         nc.sync.dma_start(offsets[:], offs)
 
         net = {}
-        for name, row, queue in (
-            ("w1_1", mlp1_w1, nc.sync),
-            ("b1_1", mlp1_b1, nc.scalar),
-            ("w2_1", mlp1_w2, nc.sync),
-            ("b2_1", mlp1_b2, nc.scalar),
-            ("w1_2", mlp2_w1, nc.sync),
-            ("b1_2", mlp2_b1, nc.scalar),
-            ("w2_2", mlp2_w2, nc.sync),
-            ("b2_2", mlp2_b2, nc.scalar),
+        for name, row in (
+            ("w1_1", mlp1_w1),
+            ("b1_1", mlp1_b1),
+            ("w2_1", mlp1_w2),
+            ("b2_1", mlp1_b2),
+            ("w1_2", mlp2_w1),
+            ("b1_2", mlp2_b1),
+            ("w2_2", mlp2_w2),
+            ("b2_2", mlp2_b2),
         ):
             width = row.shape[1]
             net[name] = held.tile([M, width], F32, name=name)
-            queue.dma_start(net[name][:], row.broadcast_to([M, width]))
+            nc.sync.dma_start(net[name][:], row.broadcast_to([M, width]))
+
+        one = held.tile([K, 1], F32, name="one")
+        nc.vector.memset(one[:], 1.0)
+        warm = held.tile([K, 1], F32, name="warm")
+        nc.scalar.activation(warm[:], one[:], ACT.Abs_reciprocal_sqrt)
 
         same_half = held.tile([K, K], BF16, name="same_half")
         nc.vector.memset(same_half[:], 0.0)
         nc.vector.memset(same_half[0:H, 0:H], 1.0)
         nc.vector.memset(same_half[H:K, H:K], 1.0)
 
-        squares = held.tile([K, S + M], BF16, name="squares")
-        nc.scalar.activation(squares[:, 0:S], table_sb[:], ACT.Square, scale=ft[:, 0:1])
-        nc.scalar.activation(squares[:, S : S + M], w_sb[:], ACT.Square, scale=fw[:, 0:1])
-
-        sums = psum.tile([K, S + M], F32, name="sums")
-        nc.tensor.matmul(sums[:], same_half[:], squares[:], start=True, stop=True)
-        inv_norm = held.tile([K, S + M], F32, name="inv_norm")
-        nc.scalar.activation(inv_norm[:], sums[:], ACT.Abs_reciprocal_sqrt)
-
         tn = held.tile([K, S], BF16, name="tn")
-        nc.vector.scalar_tensor_tensor(
-            tn[:], table_sb[:], ft[:, 0:1], inv_norm[:, 0:S], ALU.mult, ALU.mult
-        )
         wn = held.tile([K, M], BF16, name="wn")
-        nc.vector.scalar_tensor_tensor(
-            wn[:], w_sb[:], fw[:, 0:1], inv_norm[:, S : S + M], ALU.mult, ALU.mult
-        )
 
-        x = psum.tile([M, N], F32, name="x")
+        def normalise(normed, raw, scale):
+            squares = pieces.tile([K, PIECE], BF16, name="squares")
+            nc.scalar.activation(squares[:], raw, ACT.Square, scale=scale[:, 0:1])
+            sums = psum_sums.tile([K, PIECE], F32, name="sums")
+            nc.tensor.matmul(sums[:], same_half[:], squares[:], start=True, stop=True)
+            inv_norm = pieces.tile([K, PIECE], F32, name="inv_norm")
+            nc.scalar.activation(inv_norm[:], sums[:], ACT.Abs_reciprocal_sqrt)
+            nc.vector.scalar_tensor_tensor(
+                normed, raw, scale[:, 0:1], inv_norm[:], ALU.mult, ALU.mult
+            )
+
+        normalise(wn[:], w_sb[:], fw)
+        for first in range(0, S, PIECE):
+            normalise(tn[:, first : first + PIECE], table_sb[:, first : first + PIECE], ft)
+
+        x = psum_x.tile([M, N], F32, name="x")
         nc.tensor.matmul(x[:], wn[:], tn[:].indirect(offsets[:]), start=True, stop=True)
 
         def network(result, v, w1, b1, w2, b2):
@@ -115,7 +122,9 @@ def tile_maa_kernel(
                     nc.vector.scalar_tensor_tensor(
                         acc[:], unit[:], w2[:, p : p + 1], acc[:], ALU.mult, ALU.add
                     )
-            nc.vector.tensor_tensor(result, sums[0][:], sums[1][:], ALU.add)
+            nc.vector.tensor_tensor(sums[0][:], sums[0][:], sums[1][:], ALU.add)
+            nc.vector.tensor_tensor(sums[2][:], sums[2][:], sums[3][:], ALU.add)
+            nc.vector.tensor_tensor(result, sums[0][:], sums[2][:], ALU.add)
 
         h = held.tile([M, N], F32, name="h")
         network(h[:], x[:], net["w1_1"], net["b1_1"], net["w2_1"], net["b2_1"])

@@ -39,7 +39,7 @@ def tile_maa_kernel(
     with (
         tc.tile_pool(name="held", bufs=1) as held,
         tc.tile_pool(name="pieces", bufs=3) as pieces,
-        tc.tile_pool(name="units", bufs=6) as units,
+        tc.tile_pool(name="units", bufs=12) as units,
         tc.tile_pool(name="partial", bufs=2) as partial,
         tc.psum_pool(name="psum_sums", bufs=3) as psum_sums,
         tc.psum_pool(name="psum_x", bufs=1) as psum_x,
@@ -73,6 +73,14 @@ def tile_maa_kernel(
             net[name] = held.tile([M, width], F32, name=name)
             nc.sync.dma_start(net[name][:], row.broadcast_to([M, width]))
 
+        for n in ("1", "2"):
+            net["neg_b1_" + n] = held.tile([M, PHI], F32, name="neg_b1_" + n)
+            nc.gpsimd.tensor_scalar_mul(net["neg_b1_" + n][:], net["b1_" + n][:], -1.0)
+            net["w2_b1_" + n] = held.tile([M, PHI], F32, name="w2_b1_" + n)
+            nc.gpsimd.tensor_tensor(
+                net["w2_b1_" + n][:], net["w2_" + n][:], net["b1_" + n][:], ALU.mult
+            )
+
         one = held.tile([K, 1], F32, name="one")
         nc.vector.memset(one[:], 1.0)
         warm = held.tile([K, 1], F32, name="warm")
@@ -104,31 +112,36 @@ def tile_maa_kernel(
         x = psum_x.tile([M, N], F32, name="x")
         nc.tensor.matmul(x[:], wn[:], tn[:].indirect(offsets[:]), start=True, stop=True)
 
-        def network(result, v, w1, b1, w2, b2):
+        def network(result, v, n):
+            w1, b1, w2, b2 = (net[name + n] for name in ("w1_", "b1_", "w2_", "b2_"))
+            neg_b1, w2_b1 = net["neg_b1_" + n], net["w2_b1_" + n]
             sums = [partial.tile([M, N], F32, name=f"sum{c}") for c in range(CHAINS)]
-            for p in range(PHI):
+            for c in range(CHAINS):
+                nc.vector.tensor_scalar(
+                    sums[c][:], v, w1[:, c : c + 1], neg_b1[:, c : c + 1], ALU.mult, ALU.max
+                )
+            for c in range(CHAINS):
+                nc.vector.tensor_scalar(
+                    sums[c][:], sums[c][:], w2[:, c : c + 1], w2_b1[:, c : c + 1], ALU.mult, ALU.add
+                )
+            for p in range(CHAINS, PHI):
                 unit = units.tile([M, N], F32, name="unit")
                 nc.scalar.activation(
                     unit[:], v, ACT.Relu, bias=b1[:, p : p + 1], scale=w1[:, p : p + 1]
                 )
                 acc = sums[p % CHAINS]
-                if p == 0:
-                    nc.vector.tensor_scalar(
-                        acc[:], unit[:], w2[:, 0:1], b2[:, 0:1], ALU.mult, ALU.add
-                    )
-                elif p < CHAINS:
-                    nc.vector.tensor_scalar_mul(acc[:], unit[:], w2[:, p : p + 1])
-                else:
-                    nc.vector.scalar_tensor_tensor(
-                        acc[:], unit[:], w2[:, p : p + 1], acc[:], ALU.mult, ALU.add
-                    )
+                nc.vector.scalar_tensor_tensor(
+                    acc[:], unit[:], w2[:, p : p + 1], acc[:], ALU.mult, ALU.add
+                )
             nc.vector.tensor_tensor(sums[0][:], sums[0][:], sums[1][:], ALU.add)
             nc.vector.tensor_tensor(sums[2][:], sums[2][:], sums[3][:], ALU.add)
-            nc.vector.tensor_tensor(result, sums[0][:], sums[2][:], ALU.add)
+            nc.vector.scalar_tensor_tensor(
+                result, sums[0][:], b2[:, 0:1], sums[2][:], ALU.add, ALU.add
+            )
 
         h = held.tile([M, N], F32, name="h")
-        network(h[:], x[:], net["w1_1"], net["b1_1"], net["w2_1"], net["b2_1"])
+        network(h[:], x[:], "1")
         score = held.tile([M, N], F32, name="score")
-        network(score[:], h[:], net["w1_2"], net["b1_2"], net["w2_2"], net["b2_2"])
+        network(score[:], h[:], "2")
 
         nc.sync.dma_start(out, score[:])

@@ -39,7 +39,7 @@ def tile_maa_kernel(
     with (
         tc.tile_pool(name="held", bufs=1) as held,
         tc.tile_pool(name="pieces", bufs=3) as pieces,
-        tc.tile_pool(name="units", bufs=12) as units,
+        tc.tile_pool(name="units", bufs=16) as units,
         tc.tile_pool(name="partial", bufs=2) as partial,
         tc.psum_pool(name="psum_sums", bufs=3) as psum_sums,
         tc.psum_pool(name="psum_x", bufs=1) as psum_x,
@@ -73,7 +73,7 @@ def tile_maa_kernel(
             net[name] = held.tile([M, width], F32, name=name)
             nc.sync.dma_start(net[name][:], row.broadcast_to([M, width]))
 
-        for n in ("1", "2"):
+        for n in ("2",):
             net["neg_b1_" + n] = held.tile([M, PHI], F32, name="neg_b1_" + n)
             nc.gpsimd.tensor_scalar_mul(net["neg_b1_" + n][:], net["b1_" + n][:], -1.0)
             net["w2_b1_" + n] = held.tile([M, PHI], F32, name="w2_b1_" + n)
@@ -112,27 +112,30 @@ def tile_maa_kernel(
         x = psum_x.tile([M, N], F32, name="x")
         nc.tensor.matmul(x[:], wn[:], tn[:].indirect(offsets[:]), start=True, stop=True)
 
-        def network(result, v, n):
+        def network(result, v, n, own):
             w1, b1, w2, b2 = (net[name + n] for name in ("w1_", "b1_", "w2_", "b2_"))
-            neg_b1, w2_b1 = net["neg_b1_" + n], net["w2_b1_" + n]
+            neg_b1, w2_b1 = net.get("neg_b1_" + n), net.get("w2_b1_" + n)
             sums = [partial.tile([M, N], F32, name=f"sum{c}") for c in range(CHAINS)]
-            for c in range(CHAINS):
+            for c in range(own):
                 nc.vector.tensor_scalar(
                     sums[c][:], v, w1[:, c : c + 1], neg_b1[:, c : c + 1], ALU.mult, ALU.max
                 )
-            for c in range(CHAINS):
+            for c in range(own):
                 nc.vector.tensor_scalar(
                     sums[c][:], sums[c][:], w2[:, c : c + 1], w2_b1[:, c : c + 1], ALU.mult, ALU.add
                 )
-            for p in range(CHAINS, PHI):
+            for p in range(own, PHI):
                 unit = units.tile([M, N], F32, name="unit")
                 nc.scalar.activation(
                     unit[:], v, ACT.Relu, bias=b1[:, p : p + 1], scale=w1[:, p : p + 1]
                 )
                 acc = sums[p % CHAINS]
-                nc.vector.scalar_tensor_tensor(
-                    acc[:], unit[:], w2[:, p : p + 1], acc[:], ALU.mult, ALU.add
-                )
+                if p < CHAINS:
+                    nc.vector.tensor_scalar_mul(acc[:], unit[:], w2[:, p : p + 1])
+                else:
+                    nc.vector.scalar_tensor_tensor(
+                        acc[:], unit[:], w2[:, p : p + 1], acc[:], ALU.mult, ALU.add
+                    )
             nc.vector.tensor_tensor(sums[0][:], sums[0][:], sums[1][:], ALU.add)
             nc.vector.tensor_tensor(sums[2][:], sums[2][:], sums[3][:], ALU.add)
             nc.vector.scalar_tensor_tensor(
@@ -140,8 +143,8 @@ def tile_maa_kernel(
             )
 
         h = held.tile([M, N], F32, name="h")
-        network(h[:], x[:], "1")
+        network(h[:], x[:], "1", 0)
         score = held.tile([M, N], F32, name="score")
-        network(score[:], h[:], "2")
+        network(score[:], h[:], "2", CHAINS)
 
         nc.sync.dma_start(out, score[:])

@@ -39,7 +39,7 @@ def tile_maa_kernel(
     with (
         tc.tile_pool(name="held", bufs=1) as held,
         tc.tile_pool(name="pieces", bufs=3) as pieces,
-        tc.tile_pool(name="units", bufs=16) as units,
+        tc.tile_pool(name="units", bufs=PHI) as units,
         tc.tile_pool(name="partial", bufs=2) as partial,
         tc.psum_pool(name="psum_sums", bufs=3) as psum_sums,
         tc.psum_pool(name="psum_x", bufs=1) as psum_x,
@@ -73,14 +73,6 @@ def tile_maa_kernel(
             net[name] = held.tile([M, width], F32, name=name)
             nc.sync.dma_start(net[name][:], row.broadcast_to([M, width]))
 
-        for n in ("2",):
-            net["neg_b1_" + n] = held.tile([M, PHI], F32, name="neg_b1_" + n)
-            nc.gpsimd.tensor_scalar_mul(net["neg_b1_" + n][:], net["b1_" + n][:], -1.0)
-            net["w2_b1_" + n] = held.tile([M, PHI], F32, name="w2_b1_" + n)
-            nc.gpsimd.tensor_tensor(
-                net["w2_b1_" + n][:], net["w2_" + n][:], net["b1_" + n][:], ALU.mult
-            )
-
         one = held.tile([K, 1], F32, name="one")
         nc.vector.memset(one[:], 1.0)
         warm = held.tile([K, 1], F32, name="warm")
@@ -112,19 +104,9 @@ def tile_maa_kernel(
         x = psum_x.tile([M, N], F32, name="x")
         nc.tensor.matmul(x[:], wn[:], tn[:].indirect(offsets[:]), start=True, stop=True)
 
-        def network(result, v, n, own):
-            w1, b1, w2, b2 = (net[name + n] for name in ("w1_", "b1_", "w2_", "b2_"))
-            neg_b1, w2_b1 = net.get("neg_b1_" + n), net.get("w2_b1_" + n)
+        def network(result, v, w1, b1, w2, b2):
             sums = [partial.tile([M, N], F32, name=f"sum{c}") for c in range(CHAINS)]
-            for c in range(own):
-                nc.vector.tensor_scalar(
-                    sums[c][:], v, w1[:, c : c + 1], neg_b1[:, c : c + 1], ALU.mult, ALU.max
-                )
-            for c in range(own):
-                nc.vector.tensor_scalar(
-                    sums[c][:], sums[c][:], w2[:, c : c + 1], w2_b1[:, c : c + 1], ALU.mult, ALU.add
-                )
-            for p in range(own, PHI):
+            for p in range(PHI):
                 unit = units.tile([M, N], F32, name="unit")
                 nc.scalar.activation(
                     unit[:], v, ACT.Relu, bias=b1[:, p : p + 1], scale=w1[:, p : p + 1]
@@ -143,8 +125,8 @@ def tile_maa_kernel(
             )
 
         h = held.tile([M, N], F32, name="h")
-        network(h[:], x[:], "1", 0)
+        network(h[:], x[:], net["w1_1"], net["b1_1"], net["w2_1"], net["b2_1"])
         score = held.tile([M, N], F32, name="score")
-        network(score[:], h[:], "2", CHAINS)
+        network(score[:], h[:], net["w1_2"], net["b1_2"], net["w2_2"], net["b2_2"])
 
         nc.sync.dma_start(out, score[:])

@@ -12,8 +12,10 @@ S = 256
 M = 128
 N = 128
 PHI = 16
+NETWORKS = 2
 CHAINS = 4
 PIECE = 128
+PIECES = (M + S) // PIECE
 
 FLOPS = 2 * K * M * N
 
@@ -38,10 +40,10 @@ def tile_maa_kernel(
     nc = tc.nc
     with (
         tc.tile_pool(name="held", bufs=1) as held,
-        tc.tile_pool(name="pieces", bufs=3) as pieces,
+        tc.tile_pool(name="pieces", bufs=PIECES) as pieces,
         tc.tile_pool(name="units", bufs=PHI) as units,
-        tc.tile_pool(name="partial", bufs=2) as partial,
-        tc.psum_pool(name="psum_sums", bufs=3) as psum_sums,
+        tc.tile_pool(name="running", bufs=NETWORKS) as running,
+        tc.psum_pool(name="psum_pieces", bufs=PIECES) as psum_pieces,
         tc.psum_pool(name="psum_x", bufs=1) as psum_x,
     ):
         w_sb = held.tile([K, M], BF16, name="w_sb")
@@ -55,7 +57,7 @@ def tile_maa_kernel(
         nc.sync.dma_start(ft[0:H, :], fa)
         nc.sync.dma_start(ft[H:K, :], fb)
 
-        offsets = held.tile([128, N // 16], U16, name="offsets")
+        offsets = held.tile([K, N // 16], U16, name="offsets")
         nc.sync.dma_start(offsets[:], offs)
 
         net = {}
@@ -89,10 +91,10 @@ def tile_maa_kernel(
         def normalise(normed, raw, scale):
             squares = pieces.tile([K, PIECE], BF16, name="squares")
             nc.scalar.activation(squares[:], raw, ACT.Square, scale=scale[:, 0:1])
-            sums = psum_sums.tile([K, PIECE], F32, name="sums")
-            nc.tensor.matmul(sums[:], same_half[:], squares[:], start=True, stop=True)
+            half_sums = psum_pieces.tile([K, PIECE], F32, name="half_sums")
+            nc.tensor.matmul(half_sums[:], same_half[:], squares[:], start=True, stop=True)
             inv_norm = pieces.tile([K, PIECE], F32, name="inv_norm")
-            nc.scalar.activation(inv_norm[:], sums[:], ACT.Abs_reciprocal_sqrt)
+            nc.scalar.activation(inv_norm[:], half_sums[:], ACT.Abs_reciprocal_sqrt)
             nc.vector.scalar_tensor_tensor(
                 normed, raw, scale[:, 0:1], inv_norm[:], ALU.mult, ALU.mult
             )
@@ -105,7 +107,7 @@ def tile_maa_kernel(
         nc.tensor.matmul(x[:], wn[:], tn[:].indirect(offsets[:]), start=True, stop=True)
 
         def network(result, v, w1, b1, w2, b2):
-            sums = [partial.tile([M, N], F32, name=f"sum{c}") for c in range(CHAINS)]
+            sums = [running.tile([M, N], F32, name=f"sum{c}") for c in range(CHAINS)]
             for p in range(PHI):
                 unit = units.tile([M, N], F32, name="unit")
                 nc.scalar.activation(

@@ -46,16 +46,16 @@ def tile_maa_kernel(
         tc.psum_pool(name="psum_pieces", bufs=PIECES) as psum_pieces,
         tc.psum_pool(name="psum_x", bufs=1) as psum_x,
     ):
-        w_sb = held.tile([K, M], BF16, name="w_sb")
-        nc.scalar.dma_start(w_sb[:], w)
         fw = held.tile([K, 1], F32, name="fw")
         nc.scalar.dma_start(fw[0:H, :], fb)
         nc.scalar.dma_start(fw[H:K, :], fa)
-        table_sb = held.tile([K, S], BF16, name="table_sb")
-        nc.sync.dma_start(table_sb[:], table)
+        w_sb = held.tile([K, M], BF16, name="w_sb")
+        nc.scalar.dma_start(w_sb[:], w)
         ft = held.tile([K, 1], F32, name="ft")
         nc.sync.dma_start(ft[0:H, :], fa)
         nc.sync.dma_start(ft[H:K, :], fb)
+        table_sb = held.tile([K, S], BF16, name="table_sb")
+        nc.sync.dma_start(table_sb[:], table)
 
         offsets = held.tile([K, N // 16], U16, name="offsets")
         nc.sync.dma_start(offsets[:], offs)

@@ -14,6 +14,7 @@ N = 128
 PHI = 16
 NETWORKS = 2
 CHAINS = 4
+HALF = N // 2
 PIECE = 128
 PIECES = (M + S) // PIECE
 
@@ -42,6 +43,7 @@ def tile_maa_kernel(
         tc.tile_pool(name="held", bufs=1) as held,
         tc.tile_pool(name="pieces", bufs=PIECES) as pieces,
         tc.tile_pool(name="units", bufs=PHI) as units,
+        tc.tile_pool(name="half_units", bufs=PHI) as half_units,
         tc.tile_pool(name="running", bufs=NETWORKS) as running,
         tc.psum_pool(name="psum_pieces", bufs=PIECES) as psum_pieces,
         tc.psum_pool(name="psum_x", bufs=1) as psum_x,
@@ -106,29 +108,48 @@ def tile_maa_kernel(
         x = psum_x.tile([M, N], F32, name="x")
         nc.tensor.matmul(x[:], wn[:], tn[:].indirect(offsets[:]), start=True, stop=True)
 
-        def network(result, v, w1, b1, w2, b2):
+        whole = slice(0, N)
+        halves = (slice(0, HALF), slice(HALF, N))
+
+        def network(result, v, w1, b1, w2, b2, v_comes_by_halves):
+            first_units = range(0, CHAINS)
+            middle_units = range(CHAINS, PHI - CHAINS)
+            last_units = range(PHI - CHAINS, PHI)
+            steps = []
+            if v_comes_by_halves:
+                steps.extend((p, cols) for cols in halves for p in first_units)
+            else:
+                steps.extend((p, whole) for p in first_units)
+            steps.extend((p, whole) for p in middle_units)
+            steps.extend((p, cols) for cols in halves for p in last_units)
+
             sums = [running.tile([M, N], F32, name=f"sum{c}") for c in range(CHAINS)]
-            for p in range(PHI):
-                unit = units.tile([M, N], F32, name="unit")
+            for p, cols in steps:
+                if cols == whole:
+                    unit = units.tile([M, N], F32, name="unit")
+                else:
+                    unit = half_units.tile([M, HALF], F32, name="half_unit")
                 nc.scalar.activation(
-                    unit[:], v, ACT.Relu, bias=b1[:, p : p + 1], scale=w1[:, p : p + 1]
+                    unit[:], v[:, cols], ACT.Relu, bias=b1[:, p : p + 1], scale=w1[:, p : p + 1]
                 )
-                acc = sums[p % CHAINS]
+                acc = sums[p % CHAINS][:, cols]
                 if p < CHAINS:
-                    nc.vector.tensor_scalar_mul(acc[:], unit[:], w2[:, p : p + 1])
+                    nc.vector.tensor_scalar_mul(acc, unit[:], w2[:, p : p + 1])
                 else:
                     nc.vector.scalar_tensor_tensor(
-                        acc[:], unit[:], w2[:, p : p + 1], acc[:], ALU.mult, ALU.add
+                        acc, unit[:], w2[:, p : p + 1], acc, ALU.mult, ALU.add
                     )
-            nc.vector.tensor_tensor(sums[0][:], sums[0][:], sums[1][:], ALU.add)
-            nc.vector.tensor_tensor(sums[2][:], sums[2][:], sums[3][:], ALU.add)
-            nc.vector.scalar_tensor_tensor(
-                result, sums[0][:], b2[:, 0:1], sums[2][:], ALU.add, ALU.add
-            )
+            for cols in halves:
+                nc.vector.tensor_tensor(sums[0][:, cols], sums[0][:, cols], sums[1][:, cols], ALU.add)
+                nc.vector.tensor_tensor(sums[2][:, cols], sums[2][:, cols], sums[3][:, cols], ALU.add)
+            for cols in halves:
+                nc.vector.scalar_tensor_tensor(
+                    result[:, cols], sums[0][:, cols], b2[:, 0:1], sums[2][:, cols], ALU.add, ALU.add
+                )
 
         h = held.tile([M, N], F32, name="h")
-        network(h[:], x[:], net["w1_1"], net["b1_1"], net["w2_1"], net["b2_1"])
+        network(h, x, net["w1_1"], net["b1_1"], net["w2_1"], net["b2_1"], False)
         score = held.tile([M, N], F32, name="score")
-        network(score[:], h[:], net["w1_2"], net["b1_2"], net["w2_2"], net["b2_2"])
+        network(score, h, net["w1_2"], net["b1_2"], net["w2_2"], net["b2_2"], True)
 
         nc.sync.dma_start(out, score[:])

@@ -48,16 +48,16 @@ def tile_maa_kernel(
         tc.psum_pool(name="psum_pieces", bufs=PIECES) as psum_pieces,
         tc.psum_pool(name="psum_x", bufs=1) as psum_x,
     ):
-        fw = held.tile([K, 1], F32, name="fw")
-        nc.scalar.dma_start(fw[0:H, :], fb)
-        nc.scalar.dma_start(fw[H:K, :], fa)
+        ft = held.tile([K, 1], F32, name="ft")
+        nc.scalar.dma_start(ft[0:H, :], fa)
+        nc.scalar.dma_start(ft[H:K, :], fb)
         w_sb = held.tile([K, M], BF16, name="w_sb")
         nc.scalar.dma_start(w_sb[:], w)
-        ft = held.tile([K, 1], F32, name="ft")
-        nc.sync.dma_start(ft[0:H, :], fa)
-        nc.sync.dma_start(ft[H:K, :], fb)
         table_sb = held.tile([K, S], BF16, name="table_sb")
         nc.sync.dma_start(table_sb[:], table)
+        fw = held.tile([K, 1], F32, name="fw")
+        nc.sync.dma_start(fw[0:H, :], fb)
+        nc.sync.dma_start(fw[H:K, :], fa)
 
         offsets = held.tile([K, N // 16], U16, name="offsets")
         nc.sync.dma_start(offsets[:], offs)
@@ -101,9 +101,9 @@ def tile_maa_kernel(
                 normed, raw, scale[:, 0:1], inv_norm[:], ALU.mult, ALU.mult
             )
 
-        normalise(wn[:], w_sb[:], fw)
         for first in range(0, S, PIECE):
             normalise(tn[:, first : first + PIECE], table_sb[:, first : first + PIECE], ft)
+        normalise(wn[:], w_sb[:], fw)
 
         x = psum_x.tile([M, N], F32, name="x")
         nc.tensor.matmul(x[:], wn[:], tn[:].indirect(offsets[:]), start=True, stop=True)

@@ -49,15 +49,15 @@ def tile_maa_kernel(
         tc.psum_pool(name="psum_x", bufs=1) as psum_x,
     ):
         ft = held.tile([K, 1], F32, name="ft")
-        nc.scalar.dma_start(ft[0:H, :], fa)
-        nc.scalar.dma_start(ft[H:K, :], fb)
-        w_sb = held.tile([K, M], BF16, name="w_sb")
-        nc.scalar.dma_start(w_sb[:], w)
-        table_sb = held.tile([K, S], BF16, name="table_sb")
-        nc.sync.dma_start(table_sb[:], table)
         fw = held.tile([K, 1], F32, name="fw")
-        nc.sync.dma_start(fw[0:H, :], fb)
+        table_sb = held.tile([K, S], BF16, name="table_sb")
+        w_sb = held.tile([K, M], BF16, name="w_sb")
+        nc.sync.dma_start(ft[0:H, :], fa)
+        nc.scalar.dma_start(ft[H:K, :], fb)
+        nc.sync.dma_start(table_sb[:], table)
+        nc.scalar.dma_start(fw[0:H, :], fb)
         nc.sync.dma_start(fw[H:K, :], fa)
+        nc.scalar.dma_start(w_sb[:], w)
 
         offsets = held.tile([K, N // 16], U16, name="offsets")
         nc.sync.dma_start(offsets[:], offs)

@@ -75,7 +75,8 @@ def tile_maa_kernel(
         ):
             width = row.shape[1]
             net[name] = held.tile([M, width], F32, name=name)
-            nc.sync.dma_start(net[name][:], row.broadcast_to([M, width]))
+            queue = nc.gpsimd if name == "b1_1" else nc.sync
+            queue.dma_start(net[name][:], row.broadcast_to([M, width]))
 
         one = held.tile([K, 1], F32, name="one")
         nc.vector.memset(one[:], 1.0)

import concourse.mybir as mybir

F32 = mybir.dt.float32
BF16 = mybir.dt.bfloat16
U16 = mybir.dt.uint16
ACT = mybir.ActivationFunctionType
ALU = mybir.AluOpType

K = 128
H = 64
S = 256
M = 128
N = 128
PHI = 16
NETWORKS = 2
CHAINS = 4
HALF = N // 2
PIECE = 128
PIECES = (M + S) // PIECE

FLOPS = 2 * K * M * N


def tile_maa_kernel(
    tc,
    table,
    w,
    fa,
    fb,
    mlp1_w1,
    mlp1_b1,
    mlp1_w2,
    mlp1_b2,
    mlp2_w1,
    mlp2_b1,
    mlp2_w2,
    mlp2_b2,
    offs,
    out,
):
    nc = tc.nc
    with (
        tc.tile_pool(name="held", bufs=1) as held,
        tc.tile_pool(name="pieces", bufs=PIECES) as pieces,
        tc.tile_pool(name="units", bufs=PHI) as units,
        tc.tile_pool(name="half_units", bufs=PHI) as half_units,
        tc.tile_pool(name="running", bufs=NETWORKS) as running,
        tc.psum_pool(name="psum_pieces", bufs=PIECES) as psum_pieces,
        tc.psum_pool(name="psum_x", bufs=1) as psum_x,
    ):
        ft = held.tile([K, 1], F32, name="ft")
        fw = held.tile([K, 1], F32, name="fw")
        table_sb = held.tile([K, S], BF16, name="table_sb")
        w_sb = held.tile([K, M], BF16, name="w_sb")
        nc.sync.dma_start(ft[0:H, :], fa)
        nc.scalar.dma_start(ft[H:K, :], fb)
        nc.sync.dma_start(table_sb[:], table)
        nc.scalar.dma_start(fw[0:H, :], fb)
        nc.sync.dma_start(fw[H:K, :], fa)
        nc.scalar.dma_start(w_sb[:], w)

        offsets = held.tile([K, N // 16], U16, name="offsets")
        nc.sync.dma_start(offsets[:], offs)

        net = {}
        for name, row in (
            ("w1_1", mlp1_w1),
            ("b1_1", mlp1_b1),
            ("w2_1", mlp1_w2),
            ("b2_1", mlp1_b2),
            ("w1_2", mlp2_w1),
            ("b1_2", mlp2_b1),
            ("w2_2", mlp2_w2),
            ("b2_2", mlp2_b2),
        ):
            width = row.shape[1]
            net[name] = held.tile([M, width], F32, name=name)
            queue = nc.gpsimd if name == "b1_1" else nc.sync
            queue.dma_start(net[name][:], row.broadcast_to([M, width]))

        one = held.tile([K, 1], F32, name="one")
        nc.vector.memset(one[:], 1.0)
        warm = held.tile([K, 1], F32, name="warm")
        nc.scalar.activation(warm[:], one[:], ACT.Abs_reciprocal_sqrt)

        same_half = held.tile([K, K], BF16, name="same_half")
        nc.vector.memset(same_half[:], 0.0)
        nc.vector.memset(same_half[0:H, 0:H], 1.0)
        nc.vector.memset(same_half[H:K, H:K], 1.0)

        tn = held.tile([K, S], BF16, name="tn")
        wn = held.tile([K, M], BF16, name="wn")

        def normalise(normed, raw, scale):
            squares = pieces.tile([K, PIECE], BF16, name="squares")
            nc.scalar.activation(squares[:], raw, ACT.Square, scale=scale[:, 0:1])
            half_sums = psum_pieces.tile([K, PIECE], F32, name="half_sums")
            nc.tensor.matmul(half_sums[:], same_half[:], squares[:], start=True, stop=True)
            inv_norm = pieces.tile([K, PIECE], F32, name="inv_norm")
            nc.scalar.activation(inv_norm[:], half_sums[:], ACT.Abs_reciprocal_sqrt)
            nc.vector.scalar_tensor_tensor(
                normed, raw, scale[:, 0:1], inv_norm[:], ALU.mult, ALU.mult
            )

        for first in range(0, S, PIECE):
            normalise(tn[:, first : first + PIECE], table_sb[:, first : first + PIECE], ft)
        normalise(wn[:], w_sb[:], fw)

        x = psum_x.tile([M, N], F32, name="x")
        nc.tensor.matmul(x[:], wn[:], tn[:].indirect(offsets[:]), start=True, stop=True)

        whole = slice(0, N)
        halves = (slice(0, HALF), slice(HALF, N))

        def network(result, v, w1, b1, w2, b2, v_comes_by_halves):
            first_units = range(0, CHAINS)
            middle_units = range(CHAINS, PHI - CHAINS)
            last_units = range(PHI - CHAINS, PHI)
            steps = []
            if v_comes_by_halves:
                steps.extend((p, cols) for cols in halves for p in first_units)
            else:
                steps.extend((p, whole) for p in first_units)
            steps.extend((p, whole) for p in middle_units)
            steps.extend((p, cols) for cols in halves for p in last_units)

            sums = [running.tile([M, N], F32, name=f"sum{c}") for c in range(CHAINS)]
            for p, cols in steps:
                if cols == whole:
                    unit = units.tile([M, N], F32, name="unit")
                else:
                    unit = half_units.tile([M, HALF], F32, name="half_unit")
                nc.scalar.activation(
                    unit[:], v[:, cols], ACT.Relu, bias=b1[:, p : p + 1], scale=w1[:, p : p + 1]
                )
                acc = sums[p % CHAINS][:, cols]
                if p < CHAINS:
                    nc.vector.tensor_scalar_mul(acc, unit[:], w2[:, p : p + 1])
                else:
                    nc.vector.scalar_tensor_tensor(
                        acc, unit[:], w2[:, p : p + 1], acc, ALU.mult, ALU.add
                    )
            for cols in halves:
                nc.vector.tensor_tensor(sums[0][:, cols], sums[0][:, cols], sums[1][:, cols], ALU.add)
                nc.vector.tensor_tensor(sums[2][:, cols], sums[2][:, cols], sums[3][:, cols], ALU.add)
            for cols in halves:
                nc.vector.scalar_tensor_tensor(
                    result[:, cols], sums[0][:, cols], b2[:, 0:1], sums[2][:, cols], ALU.add, ALU.add
                )

        h = held.tile([M, N], F32, name="h")
        network(h, x, net["w1_1"], net["b1_1"], net["w2_1"], net["b2_1"], False)
        score = held.tile([M, N], F32, name="score")
        network(score, h, net["w1_2"], net["b1_2"], net["w2_2"], net["b2_2"], True)

        nc.sync.dma_start(out, score[:])
